import numpy as np
import ml_dtypes

BF16 = ml_dtypes.bfloat16


def bf(x):
    return np.asarray(x, np.float32).astype(BF16)


def f32(x):
    return np.asarray(x, np.float32)


def f64(x):
    return np.asarray(x).astype(np.float64)


def striped(idx):
    return np.tile(idx.reshape(-1, 16).T, (8, 1))


B, F, E, D, S, M, N = 32, 32, 16, 128, 1024, 512, 256


def setup_inputs():
    return {"faces": bf(np.random.standard_normal((D, S))), "ner": bf(np.random.standard_normal((D, M)) / np.sqrt(D)), "offs": striped(np.random.permutation(S)[:N])}


def reference(faces, ner, offs):
    idx = offs[:16].T.reshape(-1)
    return np.maximum(f64(ner).T @ f64(faces)[:, idx], 0.0)

@@ -1,0 +1,39 @@
+import concourse.mybir as mybir
+
+BF16, F32, U16 = mybir.dt.bfloat16, mybir.dt.float32, mybir.dt.uint16
+
+P = 128
+S = 1024
+M = 512
+N = 256
+BLOCKS = M // P
+
+FLOPS = 2 * P * M * N
+BYTES = P * N * 2 + P * M * 2 + P * (N // 16) * 2 + M * N * 4
+
+
+def tile_globalrankloss_kernel(tc, faces, ner, offs, out):
+    nc = tc.nc
+    with (
+        tc.tile_pool(name="held", bufs=1) as held,
+        tc.psum_pool(name="psum", bufs=1) as psum,
+    ):
+        offsets = held.tile([P, N // 16], U16, name="offsets")
+        nc.sync.dma_start(offsets[:], offs)
+        faces_sb = held.tile([P, S], BF16, name="faces_sb")
+        nc.sync.dma_start(faces_sb[:], faces)
+        ner_sb = held.tile([P, M], BF16, name="ner_sb")
+        nc.sync.dma_start(ner_sb[:], ner)
+
+        for b in range(BLOCKS):
+            sims = psum.tile([P, N], F32, name=f"sims{b}")
+            nc.tensor.matmul(
+                sims[:],
+                ner_sb[:, b * P : (b + 1) * P],
+                faces_sb[:].indirect(offsets[:]),
+                start=True,
+                stop=True,
+            )
+            rectified = held.tile([P, N], F32, name=f"rectified{b}")
+            nc.vector.tensor_scalar_max(rectified[:], sims[:], 0.0)
+            nc.sync.dma_start(out[b * P : (b + 1) * P, :], rectified[:])

@@ -21,7 +21,7 @@ def tile_globalrankloss_kernel(tc, faces, ner, offs, out):
         offsets = held.tile([P, N // 16], U16, name="offsets")
         nc.sync.dma_start(offsets[:], offs)
         faces_sb = held.tile([P, S], BF16, name="faces_sb")
-        nc.sync.dma_start(faces_sb[:], faces)
+        nc.scalar.dma_start(faces_sb[:], faces)
         ner_sb = held.tile([P, M], BF16, name="ner_sb")
         nc.sync.dma_start(ner_sb[:], ner)
 
@@ -36,4 +36,5 @@ def tile_globalrankloss_kernel(tc, faces, ner, offs, out):
             )
             rectified = held.tile([P, N], F32, name=f"rectified{b}")
             nc.vector.tensor_scalar_max(rectified[:], sims[:], 0.0)
-            nc.sync.dma_start(out[b * P : (b + 1) * P, :], rectified[:])
+            store_queue = nc.sync if b % 2 == 0 else nc.scalar
+            store_queue.dma_start(out[b * P : (b + 1) * P, :], rectified[:])

@@ -7,6 +7,8 @@ S = 1024
 M = 512
 N = 256
 BLOCKS = M // P
+BANK = 512
+WARM_UP_MATMULS = 4
 
 FLOPS = 2 * P * M * N
 BYTES = P * N * 2 + P * M * 2 + P * (N // 16) * 2 + M * N * 4
@@ -24,6 +26,12 @@ def tile_globalrankloss_kernel(tc, faces, ner, offs, out):
         nc.scalar.dma_start(faces_sb[:], faces)
         ner_sb = held.tile([P, M], BF16, name="ner_sb")
         nc.sync.dma_start(ner_sb[:], ner)
+
+        zeros = held.tile([P, BANK], BF16, name="zeros")
+        nc.vector.memset(zeros[:], 0.0)
+        unused = psum.tile([P, BANK], F32, name="unused")
+        for w in range(WARM_UP_MATMULS):
+            nc.tensor.matmul(unused[:], zeros[:, 0:P], zeros[:], start=True, stop=True)
 
         for b in range(BLOCKS):
             sims = psum.tile([P, N], F32, name=f"sims{b}")

@@ -1,14 +1,13 @@
 import concourse.mybir as mybir
 
 BF16, F32, U16 = mybir.dt.bfloat16, mybir.dt.float32, mybir.dt.uint16
+RELU = mybir.ActivationFunctionType.Relu
 
 P = 128
 S = 1024
 M = 512
 N = 256
 BLOCKS = M // P
-BANK = 512
-WARM_UP_MATMULS = 4
 
 FLOPS = 2 * P * M * N
 BYTES = P * N * 2 + P * M * 2 + P * (N // 16) * 2 + M * N * 4
@@ -21,17 +20,12 @@ def tile_globalrankloss_kernel(tc, faces, ner, offs, out):
         tc.psum_pool(name="psum", bufs=1) as psum,
     ):
         offsets = held.tile([P, N // 16], U16, name="offsets")
-        nc.sync.dma_start(offsets[:], offs)
         faces_sb = held.tile([P, S], BF16, name="faces_sb")
-        nc.scalar.dma_start(faces_sb[:], faces)
         ner_sb = held.tile([P, M], BF16, name="ner_sb")
-        nc.sync.dma_start(ner_sb[:], ner)
-
-        zeros = held.tile([P, BANK], BF16, name="zeros")
-        nc.vector.memset(zeros[:], 0.0)
-        unused = psum.tile([P, BANK], F32, name="unused")
-        for w in range(WARM_UP_MATMULS):
-            nc.tensor.matmul(unused[:], zeros[:, 0:P], zeros[:], start=True, stop=True)
+        nc.sync.dma_start(offsets[:], offs)
+        nc.sync.dma_start(ner_sb[:, 0:P], ner[:, 0:P])
+        nc.sync.dma_start(faces_sb[:], faces)
+        nc.sync.dma_start(ner_sb[:, P:M], ner[:, P:M])
 
         for b in range(BLOCKS):
             sims = psum.tile([P, N], F32, name=f"sims{b}")
@@ -43,6 +37,9 @@ def tile_globalrankloss_kernel(tc, faces, ner, offs, out):
                 stop=True,
             )
             rectified = held.tile([P, N], F32, name=f"rectified{b}")
-            nc.vector.tensor_scalar_max(rectified[:], sims[:], 0.0)
-            store_queue = nc.sync if b % 2 == 0 else nc.scalar
-            store_queue.dma_start(out[b * P : (b + 1) * P, :], rectified[:])
+            if b % 2 == 0:
+                nc.vector.tensor_scalar_max(rectified[:], sims[:], 0.0)
+                nc.sync.dma_start(out[b * P : (b + 1) * P, :], rectified[:])
+            else:
+                nc.scalar.activation(rectified[:], sims[:], RELU)
+                nc.scalar.dma_start(out[b * P : (b + 1) * P, :], rectified[:])

@@ -22,9 +22,9 @@ def tile_globalrankloss_kernel(tc, faces, ner, offs, out):
         offsets = held.tile([P, N // 16], U16, name="offsets")
         faces_sb = held.tile([P, S], BF16, name="faces_sb")
         ner_sb = held.tile([P, M], BF16, name="ner_sb")
+        nc.sync.dma_start(faces_sb[:], faces)
         nc.sync.dma_start(offsets[:], offs)
         nc.sync.dma_start(ner_sb[:, 0:P], ner[:, 0:P])
-        nc.sync.dma_start(faces_sb[:], faces)
         nc.sync.dma_start(ner_sb[:, P:M], ner[:, P:M])
 
         for b in range(BLOCKS):

@@ -23,8 +23,8 @@ def tile_globalrankloss_kernel(tc, faces, ner, offs, out):
         faces_sb = held.tile([P, S], BF16, name="faces_sb")
         ner_sb = held.tile([P, M], BF16, name="ner_sb")
         nc.sync.dma_start(faces_sb[:], faces)
-        nc.sync.dma_start(offsets[:], offs)
         nc.sync.dma_start(ner_sb[:, 0:P], ner[:, 0:P])
+        nc.sync.dma_start(offsets[:], offs)
         nc.sync.dma_start(ner_sb[:, P:M], ner[:, P:M])
 
         for b in range(BLOCKS):

@@ -37,9 +37,6 @@ def tile_globalrankloss_kernel(tc, faces, ner, offs, out):
                 stop=True,
             )
             rectified = held.tile([P, N], F32, name=f"rectified{b}")
-            if b % 2 == 0:
-                nc.vector.tensor_scalar_max(rectified[:], sims[:], 0.0)
-                nc.sync.dma_start(out[b * P : (b + 1) * P, :], rectified[:])
-            else:
-                nc.scalar.activation(rectified[:], sims[:], RELU)
-                nc.scalar.dma_start(out[b * P : (b + 1) * P, :], rectified[:])
+            nc.vector.tensor_scalar_max(rectified[:], sims[:], 0.0)
+            queue = nc.sync if b % 2 == 0 else nc.scalar
+            queue.dma_start(out[b * P : (b + 1) * P, :], rectified[:])

@@ -23,7 +23,7 @@ def tile_globalrankloss_kernel(tc, faces, ner, offs, out):
         faces_sb = held.tile([P, S], BF16, name="faces_sb")
         ner_sb = held.tile([P, M], BF16, name="ner_sb")
         nc.sync.dma_start(faces_sb[:], faces)
-        nc.sync.dma_start(ner_sb[:, 0:P], ner[:, 0:P])
+        nc.scalar.dma_start(ner_sb[:, 0:P], ner[:, 0:P])
         nc.sync.dma_start(offsets[:], offs)
         nc.sync.dma_start(ner_sb[:, P:M], ner[:, P:M])
 

@@ -25,7 +25,7 @@ def tile_globalrankloss_kernel(tc, faces, ner, offs, out):
         nc.sync.dma_start(faces_sb[:], faces)
         nc.scalar.dma_start(ner_sb[:, 0:P], ner[:, 0:P])
         nc.sync.dma_start(offsets[:], offs)
-        nc.sync.dma_start(ner_sb[:, P:M], ner[:, P:M])
+        nc.scalar.dma_start(ner_sb[:, P:M], ner[:, P:M])
 
         for b in range(BLOCKS):
             sims = psum.tile([P, N], F32, name=f"sims{b}")

@@ -22,8 +22,8 @@ def tile_globalrankloss_kernel(tc, faces, ner, offs, out):
         offsets = held.tile([P, N // 16], U16, name="offsets")
         faces_sb = held.tile([P, S], BF16, name="faces_sb")
         ner_sb = held.tile([P, M], BF16, name="ner_sb")
-        nc.sync.dma_start(faces_sb[:], faces)
-        nc.scalar.dma_start(ner_sb[:, 0:P], ner[:, 0:P])
+        nc.scalar.dma_start(faces_sb[:], faces)
+        nc.sync.dma_start(ner_sb[:, 0:P], ner[:, 0:P])
         nc.sync.dma_start(offsets[:], offs)
         nc.scalar.dma_start(ner_sb[:, P:M], ner[:, P:M])
 

@@ -27,7 +27,7 @@ def tile_globalrankloss_kernel(tc, faces, ner, offs, out):
         nc.sync.dma_start(offsets[:], offs)
         nc.scalar.dma_start(ner_sb[:, P:M], ner[:, P:M])
 
-        for b in range(BLOCKS):
+        for b in range(BLOCKS - 1):
             sims = psum.tile([P, N], F32, name=f"sims{b}")
             nc.tensor.matmul(
                 sims[:],
@@ -37,6 +37,27 @@ def tile_globalrankloss_kernel(tc, faces, ner, offs, out):
                 stop=True,
             )
             rectified = held.tile([P, N], F32, name=f"rectified{b}")
-            nc.vector.tensor_scalar_max(rectified[:], sims[:], 0.0)
-            queue = nc.sync if b % 2 == 0 else nc.scalar
-            queue.dma_start(out[b * P : (b + 1) * P, :], rectified[:])
+            if b % 2 == 0:
+                nc.vector.tensor_scalar_max(rectified[:], sims[:], 0.0)
+                nc.sync.dma_start(out[b * P : (b + 1) * P, :], rectified[:])
+            else:
+                nc.scalar.activation(rectified[:], sims[:], RELU)
+                nc.scalar.dma_start(out[b * P : (b + 1) * P, :], rectified[:])
+
+        last = held.tile([P, N], F32, name="last")
+        for half in range(2):
+            listed = slice(half * N // 2, (half + 1) * N // 2)
+            columns = slice(half * N // 32, (half + 1) * N // 32)
+            half_sims = psum.tile([P, N // 2], F32, name=f"half_sims{half}")
+            nc.tensor.matmul(
+                half_sims[:],
+                ner_sb[:, M - P : M],
+                faces_sb[:].indirect(offsets[:, columns]),
+                start=True,
+                stop=True,
+            )
+            if half == 0:
+                nc.vector.tensor_scalar_max(last[:, listed], half_sims[:], 0.0)
+            else:
+                nc.scalar.activation(last[:, listed], half_sims[:], RELU)
+        nc.scalar.dma_start(out[M - P : M, :], last[:])

import concourse.mybir as mybir

BF16, F32, U16 = mybir.dt.bfloat16, mybir.dt.float32, mybir.dt.uint16
RELU = mybir.ActivationFunctionType.Relu

P = 128
S = 1024
M = 512
N = 256
BLOCKS = M // P

FLOPS = 2 * P * M * N
BYTES = P * N * 2 + P * M * 2 + P * (N // 16) * 2 + M * N * 4


def tile_globalrankloss_kernel(tc, faces, ner, offs, out):
    nc = tc.nc
    with (
        tc.tile_pool(name="held", bufs=1) as held,
        tc.psum_pool(name="psum", bufs=1) as psum,
    ):
        offsets = held.tile([P, N // 16], U16, name="offsets")
        faces_sb = held.tile([P, S], BF16, name="faces_sb")
        ner_sb = held.tile([P, M], BF16, name="ner_sb")
        nc.scalar.dma_start(faces_sb[:], faces)
        nc.sync.dma_start(ner_sb[:, 0:P], ner[:, 0:P])
        nc.sync.dma_start(offsets[:], offs)
        nc.scalar.dma_start(ner_sb[:, P:M], ner[:, P:M])

        for b in range(BLOCKS - 1):
            sims = psum.tile([P, N], F32, name=f"sims{b}")
            nc.tensor.matmul(
                sims[:],
                ner_sb[:, b * P : (b + 1) * P],
                faces_sb[:].indirect(offsets[:]),
                start=True,
                stop=True,
            )
            rectified = held.tile([P, N], F32, name=f"rectified{b}")
            if b % 2 == 0:
                nc.vector.tensor_scalar_max(rectified[:], sims[:], 0.0)
                nc.sync.dma_start(out[b * P : (b + 1) * P, :], rectified[:])
            else:
                nc.scalar.activation(rectified[:], sims[:], RELU)
                nc.scalar.dma_start(out[b * P : (b + 1) * P, :], rectified[:])

        last = held.tile([P, N], F32, name="last")
        for half in range(2):
            listed = slice(half * N // 2, (half + 1) * N // 2)
            columns = slice(half * N // 32, (half + 1) * N // 32)
            half_sims = psum.tile([P, N // 2], F32, name=f"half_sims{half}")
            nc.tensor.matmul(
                half_sims[:],
                ner_sb[:, M - P : M],
                faces_sb[:].indirect(offsets[:, columns]),
                start=True,
                stop=True,
            )
            if half == 0:
                nc.vector.tensor_scalar_max(last[:, listed], half_sims[:], 0.0)
            else:
                nc.scalar.activation(last[:, listed], half_sims[:], RELU)
        nc.scalar.dma_start(out[M - P : M, :], last[:])
